import numpy as np
import ml_dtypes


def mxq(x, axis, fmt="e4m3"):
    dtype, down = {"e4m3": (ml_dtypes.float8_e4m3fn, 7), "e5m2": (ml_dtypes.float8_e5m2, 14)}[fmt]
    v = np.moveaxis(np.asarray(x, np.float32).astype(ml_dtypes.bfloat16).astype(np.float64), axis, -1)
    blocks = v.reshape(v.shape[:-1] + (-1, 32))
    amax = np.abs(blocks).max(-1, keepdims=True)
    byte = np.maximum(np.where(amax > 0, np.frexp(amax)[1] - 1 + 127, 0) - down, 1)
    scale = np.exp2(byte - 127.0)
    codes = (blocks / scale).astype(np.float32).astype(dtype).astype(np.float64)
    return np.moveaxis((codes * scale).reshape(v.shape), -1, axis)


WIDE = False


def mx_kscale(k):
    if not WIDE:
        return np.ones(k)
    levels = np.array([10, -10, 5, -5, 0])
    a = np.random.permutation(np.resize(levels, k // 512 * 4)).reshape(k // 512, 4)
    idx = np.arange(k)
    return np.exp2(a[idx // 512, idx % 128 // 32])


BF16 = ml_dtypes.bfloat16


def bf(x):
    return np.asarray(x, np.float32).astype(BF16)


def f64(x):
    return np.asarray(x).astype(np.float64)


B, COND, D, H, K = 128, 512, 16, 1536, 128
KD = K * D


def setup_inputs():
    s = mx_kscale(COND)
    return {
        "x": bf(np.random.standard_normal((B, COND)) * s),
        "W1": bf(np.random.standard_normal((COND, H)) * 0.8 / np.sqrt(COND) / s[:, None]),
        "b1": bf(np.random.standard_normal(H) * 0.3),
        "Wpi": bf(np.random.standard_normal((H, K)) * 3.5 / np.sqrt(H)),
        "bpi": bf(np.random.standard_normal(K) * 0.5),
        "Wsig": bf(np.random.standard_normal((H, KD)) * 1.0 / np.sqrt(H)),
        "bsig": bf(np.random.standard_normal(KD) * 0.3),
        "Wmu": bf(np.random.standard_normal((H, KD)) * 1.5 / np.sqrt(H)),
        "bmu": bf(np.random.standard_normal(KD) * 0.3),
    }


def reference(x, W1, b1, Wpi, bpi, Wsig, bsig, Wmu, bmu):
    z_h = np.tanh((mxq(f64(x), 1, "e4m3") @ mxq(f64(W1), 0, "e4m3")) + f64(b1))
    zq = mxq(z_h, 1, "e4m3")
    logits = (zq @ mxq(f64(Wpi), 0, "e4m3")) + f64(bpi)
    e = np.exp(logits - logits.max(-1, keepdims=True))
    pi = e / e.sum(-1, keepdims=True)
    sigma_diag = np.exp((zq @ mxq(f64(Wsig), 0, "e4m3")) + f64(bsig)).reshape(x.shape[0], K, D)
    sigma = sigma_diag[..., :, None] * np.eye(D)
    mu = ((zq @ mxq(f64(Wmu), 0, "e4m3")) + f64(bmu)).reshape(x.shape[0], K, D)
    return pi, sigma, mu

@@ -1,0 +1,292 @@
+from contextlib import ExitStack
+
+import concourse.mybir as mybir
+from concourse.masks import make_identity
+
+F32 = mybir.dt.float32
+BF16 = mybir.dt.bfloat16
+U32 = mybir.dt.uint32
+U8 = mybir.dt.uint8
+I32 = mybir.dt.int32
+FP8X4 = mybir.dt.float8_e4m3fn_x4
+ACT = mybir.ActivationFunctionType
+ALU = mybir.AluOpType
+AXIS = mybir.AxisListType
+
+P = 128
+PACK = 4
+K_PASS = P * PACK
+
+TOKENS = 128
+COND = 512
+HIDDEN = 1536
+COMPONENTS = 128
+DIMS = 16
+HEAD_COLS = COMPONENTS * DIMS
+HIDDEN_PASSES = HIDDEN // K_PASS
+
+BANK_COLS = 512
+HEAD_BANKS = HEAD_COLS // BANK_COLS
+
+CHUNK_COMPONENTS = 16
+CHUNK_DIAG = CHUNK_COMPONENTS * DIMS
+CHUNK_COLS = CHUNK_DIAG * DIMS
+SIGMA_CHUNKS = COMPONENTS // CHUNK_COMPONENTS
+SIGMA_BUFS = 4
+
+BSIG_AT = 0
+BMU_AT = HEAD_COLS
+BPI_AT = 2 * HEAD_COLS
+BIAS_COLS = 2 * HEAD_COLS + COMPONENTS
+
+FLOPS = 2 * TOKENS * (COND * HIDDEN + HIDDEN * (COMPONENTS + 2 * HEAD_COLS))
+
+
+def tile_mdn_pa_kernel(
+    tc, x, W1, b1, Wpi, bpi, Wsig, bsig, Wmu, bmu, out_0, out_1, out_2
+):
+    nc = tc.nc
+    with ExitStack() as stack:
+        const = stack.enter_context(tc.tile_pool(name="const", bufs=1))
+        raw_pool = stack.enter_context(tc.tile_pool(name="raw_pool", bufs=4))
+        piece_pool = stack.enter_context(tc.tile_pool(name="piece_pool", bufs=4))
+        z_pool = stack.enter_context(tc.tile_pool(name="z_pool", bufs=HIDDEN_PASSES))
+        psum = stack.enter_context(tc.psum_pool(name="psum", bufs=8))
+
+        def load_pass(weight, g, cols):
+            raw = raw_pool.tile([P, PACK, cols], BF16, tag="raw")
+            nc.sync.dma_start(
+                out=raw[:],
+                in_=weight[g * K_PASS : (g + 1) * K_PASS, :].rearrange(
+                    "(p j) n -> p j n", j=PACK
+                ),
+            )
+            return raw
+
+        x_sb = const.tile([P, COND], BF16)
+        nc.sync.dma_start(out=x_sb[:], in_=x)
+        b1_bf = const.tile([P, HIDDEN_PASSES, PACK], BF16)
+        nc.sync.dma_start(
+            out=b1_bf[:], in_=b1.rearrange("(g q t) -> q g t", g=HIDDEN_PASSES, t=PACK)
+        )
+        w1_raw = load_pass(W1, 0, HIDDEN)
+        wsig_raw = [load_pass(Wsig, g, HEAD_COLS) for g in range(HIDDEN_PASSES)]
+        wpi_raw = const.tile([P, HIDDEN_PASSES, PACK, COMPONENTS], BF16)
+        nc.sync.dma_start(
+            out=wpi_raw[:],
+            in_=Wpi.rearrange("(g p j) n -> p g j n", g=HIDDEN_PASSES, j=PACK),
+        )
+        wmu_raw = [load_pass(Wmu, g, HEAD_COLS) for g in range(HIDDEN_PASSES)]
+
+        ident = const.tile([P, P], F32)
+        make_identity(nc, ident[:])
+        ones = const.tile([P, P], BF16)
+        nc.vector.memset(ones[:], 1.0)
+        zero_col = const.tile([P, 1], F32)
+        nc.vector.memset(zero_col[:], 0.0)
+
+        bias_rows = const.tile([P, BIAS_COLS], BF16)
+        nc.vector.memset(bias_rows[:].bitcast(I32), 0)
+        nc.scalar.dma_start(
+            out=bias_rows[0:1, BSIG_AT : BSIG_AT + HEAD_COLS], in_=bsig.unsqueeze(0)
+        )
+        nc.scalar.dma_start(
+            out=bias_rows[0:1, BMU_AT : BMU_AT + HEAD_COLS], in_=bmu.unsqueeze(0)
+        )
+        nc.scalar.dma_start(
+            out=bias_rows[0:1, BPI_AT : BPI_AT + COMPONENTS], in_=bpi.unsqueeze(0)
+        )
+
+        sigma_bufs = [
+            const.tile([P, CHUNK_COLS], F32, name="sigma_buf%d" % i) for i in range(SIGMA_BUFS)
+        ]
+        for i in range(SIGMA_BUFS):
+            if i % 2 == 0:
+                nc.vector.memset(sigma_bufs[i][:], 0.0)
+            else:
+                nc.scalar.copy(
+                    out=sigma_bufs[i][:], in_=zero_col[:].to_broadcast([P, CHUNK_COLS])
+                )
+
+        def quantise(grouped):
+            codes = piece_pool.tile([P, BANK_COLS], U32, align_bytes=64)
+            scales = piece_pool.tile([P, BANK_COLS], U8, align_bytes=64)
+            nc.vector.quantize_mx(
+                out=codes[:].bitcast(FP8X4),
+                scales=scales[:],
+                in_=grouped[:].rearrange("p n j -> p (n j)"),
+            )
+            return codes, scales
+
+        x_words = x_sb[:].bitcast(F32).rearrange("m (p u) -> m u p", u=2)
+        xt = psum.tile([P, 2, TOKENS], F32, tag="bank")
+        for u in range(2):
+            nc.tensor.transpose(xt[:, u, :], x_words[:, u, :], ident[:])
+        x_grouped = const.tile([P, TOKENS * PACK], BF16, align_bytes=64)
+        nc.vector.tensor_copy(
+            out=x_grouped[:].bitcast(F32).rearrange("p (m u) -> p m u", u=2),
+            in_=xt[:].rearrange("p u m -> p m u"),
+        )
+        x_codes = const.tile([P, TOKENS], U32, align_bytes=64)
+        x_scales = const.tile([P, TOKENS], U8, align_bytes=64)
+        nc.vector.quantize_mx(
+            out=x_codes[:].bitcast(FP8X4), scales=x_scales[:], in_=x_grouped[:]
+        )
+
+        b1_f32 = const.tile([P, HIDDEN_PASSES * PACK], F32)
+        nc.vector.tensor_copy(out=b1_f32[:], in_=b1_bf[:].rearrange("q g t -> q (g t)"))
+
+        z_codes = const.tile([P, HIDDEN_PASSES, TOKENS], U32, align_bytes=64)
+        z_scales = const.tile([P, HIDDEN_PASSES, TOKENS], U8, align_bytes=64)
+        for g in range(HIDDEN_PASSES):
+            w1_grouped = piece_pool.tile([P, BANK_COLS, PACK], BF16, tag="grouped", align_bytes=64)
+            nc.vector.tensor_copy(
+                out=w1_grouped[:].rearrange("p (t q) j -> p t q j", t=PACK),
+                in_=w1_raw[:, :, g * K_PASS : (g + 1) * K_PASS].rearrange(
+                    "p j (q t) -> p t q j", t=PACK
+                ),
+            )
+            w1_codes, w1_scales = quantise(w1_grouped)
+            z_ps = psum.tile([P, PACK, TOKENS], F32, tag="bank")
+            z_rows = z_pool.tile([P, PACK, TOKENS], BF16)
+            for t in range(PACK):
+                block = slice(t * P, (t + 1) * P)
+                nc.tensor.matmul_mx(
+                    out=z_ps[:, t, :],
+                    lhsT=w1_codes[:, block].bitcast(FP8X4),
+                    lhsT_scale=w1_scales[:, block],
+                    rhs=x_codes[:].bitcast(FP8X4),
+                    rhs_scale=x_scales[:],
+                    start=True,
+                    stop=True,
+                )
+                nc.scalar.activation(
+                    out=z_rows[:, t, :],
+                    in_=z_ps[:, t, :],
+                    func=ACT.Tanh,
+                    bias=b1_f32[:, g * PACK + t : g * PACK + t + 1],
+                )
+            z_grouped = z_pool.tile([P, TOKENS, PACK], BF16, align_bytes=64)
+            nc.vector.tensor_copy(out=z_grouped[:], in_=z_rows[:].rearrange("p t m -> p m t"))
+            nc.vector.quantize_mx(
+                out=z_codes[:, g, :].bitcast(FP8X4),
+                scales=z_scales[:, g, :],
+                in_=z_grouped[:].rearrange("p m t -> p (m t)"),
+            )
+
+        bias_all = const.tile([P, BIAS_COLS], F32)
+        for at in range(0, BIAS_COLS, BANK_COLS):
+            width = min(BANK_COLS, BIAS_COLS - at)
+            spread = psum.tile([P, BANK_COLS], F32, tag="bank")
+            nc.tensor.matmul(
+                out=spread[:, :width],
+                lhsT=ones[:],
+                rhs=bias_rows[:, at : at + width],
+                start=True,
+                stop=True,
+            )
+            nc.scalar.copy(out=bias_all[:, at : at + width], in_=spread[:, :width])
+
+        def head_product(raw_passes, label):
+            banks = [
+                psum.tile([P, BANK_COLS], F32, tag="bank", name="%s_acc%d" % (label, c))
+                for c in range(HEAD_BANKS)
+            ]
+            for g in range(HIDDEN_PASSES):
+                for c in range(HEAD_BANKS):
+                    rows = raw_passes[g][:, :, c * BANK_COLS : (c + 1) * BANK_COLS]
+                    grouped = piece_pool.tile([P, BANK_COLS, PACK], BF16, align_bytes=64)
+                    copy = nc.vector.tensor_copy if c % 2 == 0 else nc.scalar.copy
+                    copy(
+                        out=grouped[:].rearrange("p (n i) j -> p n j i", i=4),
+                        in_=rows.rearrange("p j (n i) -> p n j i", i=4),
+                    )
+                    codes, scales = quantise(grouped)
+                    nc.tensor.matmul_mx(
+                        out=banks[c][:],
+                        lhsT=z_codes[:, g, :].bitcast(FP8X4),
+                        lhsT_scale=z_scales[:, g, :],
+                        rhs=codes[:].bitcast(FP8X4),
+                        rhs_scale=scales[:],
+                        start=(g == 0),
+                        stop=(g == HIDDEN_PASSES - 1),
+                    )
+            return banks
+
+        sigma_flat = out_1.rearrange("b k i j -> b (k i j)")
+        sig_banks = head_product(wsig_raw, "sig")
+        for c in range(HEAD_BANKS):
+            sig_pre = const.tile([P, BANK_COLS], F32, name="sig_pre%d" % c)
+            nc.vector.tensor_tensor(
+                out=sig_pre[:],
+                in0=sig_banks[c][:],
+                in1=bias_all[:, BSIG_AT + c * BANK_COLS : BSIG_AT + (c + 1) * BANK_COLS],
+                op=ALU.add,
+            )
+            for h in range(BANK_COLS // CHUNK_DIAG):
+                chunk = c * (BANK_COLS // CHUNK_DIAG) + h
+                buf = sigma_bufs[chunk % SIGMA_BUFS]
+                diagonals = buf[:].rearrange("p (k e) -> p k e", e=DIMS * DIMS)[
+                    :, :, 0 : DIMS * DIMS : DIMS + 1
+                ]
+                nc.scalar.activation(
+                    out=diagonals,
+                    in_=sig_pre[:, h * CHUNK_DIAG : (h + 1) * CHUNK_DIAG].rearrange(
+                        "p (k i) -> p k i", i=DIMS
+                    ),
+                    func=ACT.Exp,
+                )
+                nc.scalar.dma_start(
+                    out=sigma_flat[:, chunk * CHUNK_COLS : (chunk + 1) * CHUNK_COLS], in_=buf[:]
+                )
+
+        wpi_grouped = const.tile([P, HIDDEN_PASSES, COMPONENTS, PACK], BF16, align_bytes=64)
+        nc.vector.tensor_copy(out=wpi_grouped[:], in_=wpi_raw[:].rearrange("p g j n -> p g n j"))
+        wpi_codes = const.tile([P, HIDDEN_PASSES, COMPONENTS], U32, align_bytes=64)
+        wpi_scales = const.tile([P, HIDDEN_PASSES, COMPONENTS], U8, align_bytes=64)
+        pi_ps = psum.tile([P, COMPONENTS], F32, tag="bank")
+        for g in range(HIDDEN_PASSES):
+            nc.vector.quantize_mx(
+                out=wpi_codes[:, g, :].bitcast(FP8X4),
+                scales=wpi_scales[:, g, :],
+                in_=wpi_grouped[:, g, :, :].rearrange("p n j -> p (n j)"),
+            )
+            nc.tensor.matmul_mx(
+                out=pi_ps[:],
+                lhsT=z_codes[:, g, :].bitcast(FP8X4),
+                lhsT_scale=z_scales[:, g, :],
+                rhs=wpi_codes[:, g, :].bitcast(FP8X4),
+                rhs_scale=wpi_scales[:, g, :],
+                start=(g == 0),
+                stop=(g == HIDDEN_PASSES - 1),
+            )
+        logits = const.tile([P, COMPONENTS], F32)
+        nc.vector.tensor_tensor(
+            out=logits[:], in0=pi_ps[:], in1=bias_all[:, BPI_AT : BPI_AT + COMPONENTS], op=ALU.add
+        )
+        top = const.tile([P, 1], F32)
+        nc.vector.reduce_max(out=top[:], in_=logits[:], axis=AXIS.X)
+        minus_top = const.tile([P, 1], F32)
+        nc.vector.tensor_scalar_mul(out=minus_top[:], in0=top[:], scalar1=-1.0)
+        weights = const.tile([P, COMPONENTS], F32)
+        total = const.tile([P, 1], F32)
+        nc.scalar.activation(
+            out=weights[:], in_=logits[:], func=ACT.Exp, bias=minus_top[:], accum_out=total[:]
+        )
+        inverse = const.tile([P, 1], F32)
+        nc.vector.reciprocal(out=inverse[:], in_=total[:])
+        pi_sb = const.tile([P, COMPONENTS], F32)
+        nc.vector.tensor_scalar_mul(out=pi_sb[:], in0=weights[:], scalar1=inverse[:])
+        nc.sync.dma_start(out=out_0, in_=pi_sb[:])
+
+        mu_banks = head_product(wmu_raw, "mu")
+        mu_sb = const.tile([P, HEAD_COLS], F32)
+        for c in range(HEAD_BANKS):
+            cols = slice(c * BANK_COLS, (c + 1) * BANK_COLS)
+            nc.vector.tensor_tensor(
+                out=mu_sb[:, cols],
+                in0=mu_banks[c][:],
+                in1=bias_all[:, BMU_AT + c * BANK_COLS : BMU_AT + (c + 1) * BANK_COLS],
+                op=ALU.add,
+            )
+        nc.sync.dma_start(out=out_2.rearrange("b k i -> b (k i)"), in_=mu_sb[:])

@@ -27,12 +27,16 @@ HIDDEN_PASSES = HIDDEN // K_PASS
 
 BANK_COLS = 512
 HEAD_BANKS = HEAD_COLS // BANK_COLS
+UNIT_BANKS = 2
+UNIT_COLS = UNIT_BANKS * BANK_COLS
+PASS_UNITS = HEAD_COLS // UNIT_COLS
+WSIG_SCALAR_COLS = 512
 
 CHUNK_COMPONENTS = 16
 CHUNK_DIAG = CHUNK_COMPONENTS * DIMS
 CHUNK_COLS = CHUNK_DIAG * DIMS
 SIGMA_CHUNKS = COMPONENTS // CHUNK_COMPONENTS
-SIGMA_BUFS = 4
+SIGMA_BUFS = 3
 
 BSIG_AT = 0
 BMU_AT = HEAD_COLS
@@ -48,8 +52,8 @@ def tile_mdn_pa_kernel(
     nc = tc.nc
     with ExitStack() as stack:
         const = stack.enter_context(tc.tile_pool(name="const", bufs=1))
-        raw_pool = stack.enter_context(tc.tile_pool(name="raw_pool", bufs=4))
-        piece_pool = stack.enter_context(tc.tile_pool(name="piece_pool", bufs=4))
+        raw_pool = stack.enter_context(tc.tile_pool(name="raw_pool", bufs=5))
+        unit_pool = stack.enter_context(tc.tile_pool(name="unit_pool", bufs=3))
         z_pool = stack.enter_context(tc.tile_pool(name="z_pool", bufs=HIDDEN_PASSES))
         psum = stack.enter_context(tc.psum_pool(name="psum", bufs=8))
 
@@ -100,17 +104,13 @@ def tile_mdn_pa_kernel(
         sigma_bufs = [
             const.tile([P, CHUNK_COLS], F32, name="sigma_buf%d" % i) for i in range(SIGMA_BUFS)
         ]
-        for i in range(SIGMA_BUFS):
-            if i % 2 == 0:
-                nc.vector.memset(sigma_bufs[i][:], 0.0)
-            else:
-                nc.scalar.copy(
-                    out=sigma_bufs[i][:], in_=zero_col[:].to_broadcast([P, CHUNK_COLS])
-                )
+        for buf in sigma_bufs[:-1]:
+            nc.vector.memset(buf[:], 0.0)
+        nc.scalar.copy(out=sigma_bufs[-1][:], in_=zero_col[:].to_broadcast([P, CHUNK_COLS]))
 
-        def quantise(grouped):
-            codes = piece_pool.tile([P, BANK_COLS], U32, align_bytes=64)
-            scales = piece_pool.tile([P, BANK_COLS], U8, align_bytes=64)
+        def quantise(grouped, cols):
+            codes = unit_pool.tile([P, cols], U32, tag="codes", align_bytes=64)
+            scales = unit_pool.tile([P, cols], U8, tag="scales", align_bytes=64)
             nc.vector.quantize_mx(
                 out=codes[:].bitcast(FP8X4),
                 scales=scales[:],
@@ -136,17 +136,30 @@ def tile_mdn_pa_kernel(
         b1_f32 = const.tile([P, HIDDEN_PASSES * PACK], F32)
         nc.vector.tensor_copy(out=b1_f32[:], in_=b1_bf[:].rearrange("q g t -> q (g t)"))
 
+        bias_all = const.tile([P, BIAS_COLS], F32)
+        for at in range(0, BIAS_COLS, BANK_COLS):
+            width = min(BANK_COLS, BIAS_COLS - at)
+            spread = psum.tile([P, BANK_COLS], F32, tag="bank")
+            nc.tensor.matmul(
+                out=spread[:, :width],
+                lhsT=ones[:],
+                rhs=bias_rows[:, at : at + width],
+                start=True,
+                stop=True,
+            )
+            nc.scalar.copy(out=bias_all[:, at : at + width], in_=spread[:, :width])
+
         z_codes = const.tile([P, HIDDEN_PASSES, TOKENS], U32, align_bytes=64)
         z_scales = const.tile([P, HIDDEN_PASSES, TOKENS], U8, align_bytes=64)
         for g in range(HIDDEN_PASSES):
-            w1_grouped = piece_pool.tile([P, BANK_COLS, PACK], BF16, tag="grouped", align_bytes=64)
+            w1_grouped = unit_pool.tile([P, K_PASS, PACK], BF16, tag="grouped", align_bytes=64)
             nc.vector.tensor_copy(
                 out=w1_grouped[:].rearrange("p (t q) j -> p t q j", t=PACK),
                 in_=w1_raw[:, :, g * K_PASS : (g + 1) * K_PASS].rearrange(
                     "p j (q t) -> p t q j", t=PACK
                 ),
             )
-            w1_codes, w1_scales = quantise(w1_grouped)
+            w1_codes, w1_scales = quantise(w1_grouped, K_PASS)
             z_ps = psum.tile([P, PACK, TOKENS], F32, tag="bank")
             z_rows = z_pool.tile([P, PACK, TOKENS], BF16)
             for t in range(PACK):
@@ -174,47 +187,41 @@ def tile_mdn_pa_kernel(
                 in_=z_grouped[:].rearrange("p m t -> p (m t)"),
             )
 
-        bias_all = const.tile([P, BIAS_COLS], F32)
-        for at in range(0, BIAS_COLS, BANK_COLS):
-            width = min(BANK_COLS, BIAS_COLS - at)
-            spread = psum.tile([P, BANK_COLS], F32, tag="bank")
-            nc.tensor.matmul(
-                out=spread[:, :width],
-                lhsT=ones[:],
-                rhs=bias_rows[:, at : at + width],
-                start=True,
-                stop=True,
-            )
-            nc.scalar.copy(out=bias_all[:, at : at + width], in_=spread[:, :width])
-
-        def head_product(raw_passes, label):
+        def head_product(raw_passes, label, scalar_cols):
             banks = [
                 psum.tile([P, BANK_COLS], F32, tag="bank", name="%s_acc%d" % (label, c))
                 for c in range(HEAD_BANKS)
             ]
+            vector_cols = UNIT_COLS - scalar_cols
             for g in range(HIDDEN_PASSES):
-                for c in range(HEAD_BANKS):
-                    rows = raw_passes[g][:, :, c * BANK_COLS : (c + 1) * BANK_COLS]
-                    grouped = piece_pool.tile([P, BANK_COLS, PACK], BF16, align_bytes=64)
-                    copy = nc.vector.tensor_copy if c % 2 == 0 else nc.scalar.copy
-                    copy(
-                        out=grouped[:].rearrange("p (n i) j -> p n j i", i=4),
-                        in_=rows.rearrange("p j (n i) -> p n j i", i=4),
+                for u in range(PASS_UNITS):
+                    rows = raw_passes[g][:, :, u * UNIT_COLS : (u + 1) * UNIT_COLS]
+                    grouped = unit_pool.tile([P, UNIT_COLS, PACK], BF16, align_bytes=64)
+                    nc.vector.tensor_copy(
+                        out=grouped[:, :vector_cols, :].rearrange("p (n i) j -> p n j i", i=4),
+                        in_=rows[:, :, :vector_cols].rearrange("p j (n i) -> p n j i", i=4),
                     )
-                    codes, scales = quantise(grouped)
-                    nc.tensor.matmul_mx(
-                        out=banks[c][:],
-                        lhsT=z_codes[:, g, :].bitcast(FP8X4),
-                        lhsT_scale=z_scales[:, g, :],
-                        rhs=codes[:].bitcast(FP8X4),
-                        rhs_scale=scales[:],
-                        start=(g == 0),
-                        stop=(g == HIDDEN_PASSES - 1),
-                    )
+                    if scalar_cols > 0:
+                        nc.scalar.copy(
+                            out=grouped[:, vector_cols:, :].rearrange("p (n i) j -> p n j i", i=4),
+                            in_=rows[:, :, vector_cols:].rearrange("p j (n i) -> p n j i", i=4),
+                        )
+                    codes, scales = quantise(grouped, UNIT_COLS)
+                    for b in range(UNIT_BANKS):
+                        cols = slice(b * BANK_COLS, (b + 1) * BANK_COLS)
+                        nc.tensor.matmul_mx(
+                            out=banks[u * UNIT_BANKS + b][:],
+                            lhsT=z_codes[:, g, :].bitcast(FP8X4),
+                            lhsT_scale=z_scales[:, g, :],
+                            rhs=codes[:, cols].bitcast(FP8X4),
+                            rhs_scale=scales[:, cols],
+                            start=(g == 0),
+                            stop=(g == HIDDEN_PASSES - 1),
+                        )
             return banks
 
         sigma_flat = out_1.rearrange("b k i j -> b (k i j)")
-        sig_banks = head_product(wsig_raw, "sig")
+        sig_banks = head_product(wsig_raw, "sig", WSIG_SCALAR_COLS)
         for c in range(HEAD_BANKS):
             sig_pre = const.tile([P, BANK_COLS], F32, name="sig_pre%d" % c)
             nc.vector.tensor_tensor(
@@ -279,7 +286,7 @@ def tile_mdn_pa_kernel(
         nc.vector.tensor_scalar_mul(out=pi_sb[:], in0=weights[:], scalar1=inverse[:])
         nc.sync.dma_start(out=out_0, in_=pi_sb[:])
 
-        mu_banks = head_product(wmu_raw, "mu")
+        mu_banks = head_product(wmu_raw, "mu", 0)
         mu_sb = const.tile([P, HEAD_COLS], F32)
         for c in range(HEAD_BANKS):
             cols = slice(c * BANK_COLS, (c + 1) * BANK_COLS)

@@ -26,7 +26,6 @@ HEAD_COLS = COMPONENTS * DIMS
 HIDDEN_PASSES = HIDDEN // K_PASS
 
 BANK_COLS = 512
-HEAD_BANKS = HEAD_COLS // BANK_COLS
 UNIT_BANKS = 2
 UNIT_COLS = UNIT_BANKS * BANK_COLS
 PASS_UNITS = HEAD_COLS // UNIT_COLS
@@ -187,65 +186,68 @@ def tile_mdn_pa_kernel(
                 in_=z_grouped[:].rearrange("p m t -> p (m t)"),
             )
 
-        def head_product(raw_passes, label, scalar_cols):
+        def unit_product(raw_passes, u, label, scalar_cols):
             banks = [
-                psum.tile([P, BANK_COLS], F32, tag="bank", name="%s_acc%d" % (label, c))
-                for c in range(HEAD_BANKS)
+                psum.tile([P, BANK_COLS], F32, tag="bank", name="%s_acc%d" % (label, b))
+                for b in range(UNIT_BANKS)
             ]
             vector_cols = UNIT_COLS - scalar_cols
             for g in range(HIDDEN_PASSES):
-                for u in range(PASS_UNITS):
-                    rows = raw_passes[g][:, :, u * UNIT_COLS : (u + 1) * UNIT_COLS]
-                    grouped = unit_pool.tile([P, UNIT_COLS, PACK], BF16, align_bytes=64)
-                    nc.vector.tensor_copy(
-                        out=grouped[:, :vector_cols, :].rearrange("p (n i) j -> p n j i", i=4),
-                        in_=rows[:, :, :vector_cols].rearrange("p j (n i) -> p n j i", i=4),
+                rows = raw_passes[g][:, :, u * UNIT_COLS : (u + 1) * UNIT_COLS]
+                grouped = unit_pool.tile([P, UNIT_COLS, PACK], BF16, align_bytes=64)
+                nc.vector.tensor_copy(
+                    out=grouped[:, :vector_cols, :].rearrange("p (n i) j -> p n j i", i=4),
+                    in_=rows[:, :, :vector_cols].rearrange("p j (n i) -> p n j i", i=4),
+                )
+                if scalar_cols > 0:
+                    nc.scalar.copy(
+                        out=grouped[:, vector_cols:, :].rearrange("p (n i) j -> p n j i", i=4),
+                        in_=rows[:, :, vector_cols:].rearrange("p j (n i) -> p n j i", i=4),
                     )
-                    if scalar_cols > 0:
-                        nc.scalar.copy(
-                            out=grouped[:, vector_cols:, :].rearrange("p (n i) j -> p n j i", i=4),
-                            in_=rows[:, :, vector_cols:].rearrange("p j (n i) -> p n j i", i=4),
-                        )
-                    codes, scales = quantise(grouped, UNIT_COLS)
-                    for b in range(UNIT_BANKS):
-                        cols = slice(b * BANK_COLS, (b + 1) * BANK_COLS)
-                        nc.tensor.matmul_mx(
-                            out=banks[u * UNIT_BANKS + b][:],
-                            lhsT=z_codes[:, g, :].bitcast(FP8X4),
-                            lhsT_scale=z_scales[:, g, :],
-                            rhs=codes[:, cols].bitcast(FP8X4),
-                            rhs_scale=scales[:, cols],
-                            start=(g == 0),
-                            stop=(g == HIDDEN_PASSES - 1),
-                        )
+                codes, scales = quantise(grouped, UNIT_COLS)
+                for b in range(UNIT_BANKS):
+                    cols = slice(b * BANK_COLS, (b + 1) * BANK_COLS)
+                    nc.tensor.matmul_mx(
+                        out=banks[b][:],
+                        lhsT=z_codes[:, g, :].bitcast(FP8X4),
+                        lhsT_scale=z_scales[:, g, :],
+                        rhs=codes[:, cols].bitcast(FP8X4),
+                        rhs_scale=scales[:, cols],
+                        start=(g == 0),
+                        stop=(g == HIDDEN_PASSES - 1),
+                    )
             return banks
 
         sigma_flat = out_1.rearrange("b k i j -> b (k i j)")
-        sig_banks = head_product(wsig_raw, "sig", WSIG_SCALAR_COLS)
-        for c in range(HEAD_BANKS):
-            sig_pre = const.tile([P, BANK_COLS], F32, name="sig_pre%d" % c)
-            nc.vector.tensor_tensor(
-                out=sig_pre[:],
-                in0=sig_banks[c][:],
-                in1=bias_all[:, BSIG_AT + c * BANK_COLS : BSIG_AT + (c + 1) * BANK_COLS],
-                op=ALU.add,
-            )
-            for h in range(BANK_COLS // CHUNK_DIAG):
-                chunk = c * (BANK_COLS // CHUNK_DIAG) + h
-                buf = sigma_bufs[chunk % SIGMA_BUFS]
-                diagonals = buf[:].rearrange("p (k e) -> p k e", e=DIMS * DIMS)[
-                    :, :, 0 : DIMS * DIMS : DIMS + 1
-                ]
-                nc.scalar.activation(
-                    out=diagonals,
-                    in_=sig_pre[:, h * CHUNK_DIAG : (h + 1) * CHUNK_DIAG].rearrange(
-                        "p (k i) -> p k i", i=DIMS
-                    ),
-                    func=ACT.Exp,
+        bank_chunks = BANK_COLS // CHUNK_DIAG
+        for u in range(PASS_UNITS):
+            sig_banks = unit_product(wsig_raw, u, "sig", WSIG_SCALAR_COLS)
+            for b in range(UNIT_BANKS):
+                c = u * UNIT_BANKS + b
+                sig_pre = const.tile([P, BANK_COLS], F32, name="sig_pre%d" % c)
+                nc.vector.tensor_tensor(
+                    out=sig_pre[:],
+                    in0=sig_banks[b][:],
+                    in1=bias_all[:, BSIG_AT + c * BANK_COLS : BSIG_AT + (c + 1) * BANK_COLS],
+                    op=ALU.add,
                 )
-                nc.scalar.dma_start(
-                    out=sigma_flat[:, chunk * CHUNK_COLS : (chunk + 1) * CHUNK_COLS], in_=buf[:]
-                )
+                for h in range(bank_chunks):
+                    chunk = c * bank_chunks + h
+                    buf = sigma_bufs[chunk % SIGMA_BUFS]
+                    diagonals = buf[:].rearrange("p (k e) -> p k e", e=DIMS * DIMS)[
+                        :, :, 0 : DIMS * DIMS : DIMS + 1
+                    ]
+                    nc.scalar.activation(
+                        out=diagonals,
+                        in_=sig_pre[:, h * CHUNK_DIAG : (h + 1) * CHUNK_DIAG].rearrange(
+                            "p (k i) -> p k i", i=DIMS
+                        ),
+                        func=ACT.Exp,
+                    )
+                    nc.scalar.dma_start(
+                        out=sigma_flat[:, chunk * CHUNK_COLS : (chunk + 1) * CHUNK_COLS],
+                        in_=buf[:],
+                    )
 
         wpi_grouped = const.tile([P, HIDDEN_PASSES, COMPONENTS, PACK], BF16, align_bytes=64)
         nc.vector.tensor_copy(out=wpi_grouped[:], in_=wpi_raw[:].rearrange("p g j n -> p g n j"))
@@ -286,14 +288,15 @@ def tile_mdn_pa_kernel(
         nc.vector.tensor_scalar_mul(out=pi_sb[:], in0=weights[:], scalar1=inverse[:])
         nc.sync.dma_start(out=out_0, in_=pi_sb[:])
 
-        mu_banks = head_product(wmu_raw, "mu", 0)
         mu_sb = const.tile([P, HEAD_COLS], F32)
-        for c in range(HEAD_BANKS):
-            cols = slice(c * BANK_COLS, (c + 1) * BANK_COLS)
-            nc.vector.tensor_tensor(
-                out=mu_sb[:, cols],
-                in0=mu_banks[c][:],
-                in1=bias_all[:, BMU_AT + c * BANK_COLS : BMU_AT + (c + 1) * BANK_COLS],
-                op=ALU.add,
-            )
+        for u in range(PASS_UNITS):
+            mu_banks = unit_product(wmu_raw, u, "mu", 0)
+            for b in range(UNIT_BANKS):
+                c = u * UNIT_BANKS + b
+                nc.vector.tensor_tensor(
+                    out=mu_sb[:, c * BANK_COLS : (c + 1) * BANK_COLS],
+                    in0=mu_banks[b][:],
+                    in1=bias_all[:, BMU_AT + c * BANK_COLS : BMU_AT + (c + 1) * BANK_COLS],
+                    op=ALU.add,
+                )
         nc.sync.dma_start(out=out_2.rearrange("b k i -> b (k i)"), in_=mu_sb[:])

from contextlib import ExitStack

import concourse.mybir as mybir
from concourse.masks import make_identity

F32 = mybir.dt.float32
BF16 = mybir.dt.bfloat16
U32 = mybir.dt.uint32
U8 = mybir.dt.uint8
I32 = mybir.dt.int32
FP8X4 = mybir.dt.float8_e4m3fn_x4
ACT = mybir.ActivationFunctionType
ALU = mybir.AluOpType
AXIS = mybir.AxisListType

P = 128
PACK = 4
K_PASS = P * PACK

TOKENS = 128
COND = 512
HIDDEN = 1536
COMPONENTS = 128
DIMS = 16
HEAD_COLS = COMPONENTS * DIMS
HIDDEN_PASSES = HIDDEN // K_PASS

BANK_COLS = 512
UNIT_BANKS = 2
UNIT_COLS = UNIT_BANKS * BANK_COLS
PASS_UNITS = HEAD_COLS // UNIT_COLS
WSIG_SCALAR_COLS = 512

CHUNK_COMPONENTS = 16
CHUNK_DIAG = CHUNK_COMPONENTS * DIMS
CHUNK_COLS = CHUNK_DIAG * DIMS
SIGMA_CHUNKS = COMPONENTS // CHUNK_COMPONENTS
SIGMA_BUFS = 3

BSIG_AT = 0
BMU_AT = HEAD_COLS
BPI_AT = 2 * HEAD_COLS
BIAS_COLS = 2 * HEAD_COLS + COMPONENTS

FLOPS = 2 * TOKENS * (COND * HIDDEN + HIDDEN * (COMPONENTS + 2 * HEAD_COLS))


def tile_mdn_pa_kernel(
    tc, x, W1, b1, Wpi, bpi, Wsig, bsig, Wmu, bmu, out_0, out_1, out_2
):
    nc = tc.nc
    with ExitStack() as stack:
        const = stack.enter_context(tc.tile_pool(name="const", bufs=1))
        raw_pool = stack.enter_context(tc.tile_pool(name="raw_pool", bufs=5))
        unit_pool = stack.enter_context(tc.tile_pool(name="unit_pool", bufs=3))
        z_pool = stack.enter_context(tc.tile_pool(name="z_pool", bufs=HIDDEN_PASSES))
        psum = stack.enter_context(tc.psum_pool(name="psum", bufs=8))

        def load_pass(weight, g, cols):
            raw = raw_pool.tile([P, PACK, cols], BF16, tag="raw")
            nc.sync.dma_start(
                out=raw[:],
                in_=weight[g * K_PASS : (g + 1) * K_PASS, :].rearrange(
                    "(p j) n -> p j n", j=PACK
                ),
            )
            return raw

        x_sb = const.tile([P, COND], BF16)
        nc.sync.dma_start(out=x_sb[:], in_=x)
        b1_bf = const.tile([P, HIDDEN_PASSES, PACK], BF16)
        nc.sync.dma_start(
            out=b1_bf[:], in_=b1.rearrange("(g q t) -> q g t", g=HIDDEN_PASSES, t=PACK)
        )
        w1_raw = load_pass(W1, 0, HIDDEN)
        wsig_raw = [load_pass(Wsig, g, HEAD_COLS) for g in range(HIDDEN_PASSES)]
        wpi_raw = const.tile([P, HIDDEN_PASSES, PACK, COMPONENTS], BF16)
        nc.sync.dma_start(
            out=wpi_raw[:],
            in_=Wpi.rearrange("(g p j) n -> p g j n", g=HIDDEN_PASSES, j=PACK),
        )
        wmu_raw = [load_pass(Wmu, g, HEAD_COLS) for g in range(HIDDEN_PASSES)]

        ident = const.tile([P, P], F32)
        make_identity(nc, ident[:])
        ones = const.tile([P, P], BF16)
        nc.vector.memset(ones[:], 1.0)
        zero_col = const.tile([P, 1], F32)
        nc.vector.memset(zero_col[:], 0.0)

        bias_rows = const.tile([P, BIAS_COLS], BF16)
        nc.vector.memset(bias_rows[:].bitcast(I32), 0)
        nc.scalar.dma_start(
            out=bias_rows[0:1, BSIG_AT : BSIG_AT + HEAD_COLS], in_=bsig.unsqueeze(0)
        )
        nc.scalar.dma_start(
            out=bias_rows[0:1, BMU_AT : BMU_AT + HEAD_COLS], in_=bmu.unsqueeze(0)
        )
        nc.scalar.dma_start(
            out=bias_rows[0:1, BPI_AT : BPI_AT + COMPONENTS], in_=bpi.unsqueeze(0)
        )

        sigma_bufs = [
            const.tile([P, CHUNK_COLS], F32, name="sigma_buf%d" % i) for i in range(SIGMA_BUFS)
        ]
        for buf in sigma_bufs[:-1]:
            nc.vector.memset(buf[:], 0.0)
        nc.scalar.copy(out=sigma_bufs[-1][:], in_=zero_col[:].to_broadcast([P, CHUNK_COLS]))

        def quantise(grouped, cols):
            codes = unit_pool.tile([P, cols], U32, tag="codes", align_bytes=64)
            scales = unit_pool.tile([P, cols], U8, tag="scales", align_bytes=64)
            nc.vector.quantize_mx(
                out=codes[:].bitcast(FP8X4),
                scales=scales[:],
                in_=grouped[:].rearrange("p n j -> p (n j)"),
            )
            return codes, scales

        x_words = x_sb[:].bitcast(F32).rearrange("m (p u) -> m u p", u=2)
        xt = psum.tile([P, 2, TOKENS], F32, tag="bank")
        for u in range(2):
            nc.tensor.transpose(xt[:, u, :], x_words[:, u, :], ident[:])
        x_grouped = const.tile([P, TOKENS * PACK], BF16, align_bytes=64)
        nc.vector.tensor_copy(
            out=x_grouped[:].bitcast(F32).rearrange("p (m u) -> p m u", u=2),
            in_=xt[:].rearrange("p u m -> p m u"),
        )
        x_codes = const.tile([P, TOKENS], U32, align_bytes=64)
        x_scales = const.tile([P, TOKENS], U8, align_bytes=64)
        nc.vector.quantize_mx(
            out=x_codes[:].bitcast(FP8X4), scales=x_scales[:], in_=x_grouped[:]
        )

        b1_f32 = const.tile([P, HIDDEN_PASSES * PACK], F32)
        nc.vector.tensor_copy(out=b1_f32[:], in_=b1_bf[:].rearrange("q g t -> q (g t)"))

        bias_all = const.tile([P, BIAS_COLS], F32)
        for at in range(0, BIAS_COLS, BANK_COLS):
            width = min(BANK_COLS, BIAS_COLS - at)
            spread = psum.tile([P, BANK_COLS], F32, tag="bank")
            nc.tensor.matmul(
                out=spread[:, :width],
                lhsT=ones[:],
                rhs=bias_rows[:, at : at + width],
                start=True,
                stop=True,
            )
            nc.scalar.copy(out=bias_all[:, at : at + width], in_=spread[:, :width])

        z_codes = const.tile([P, HIDDEN_PASSES, TOKENS], U32, align_bytes=64)
        z_scales = const.tile([P, HIDDEN_PASSES, TOKENS], U8, align_bytes=64)
        for g in range(HIDDEN_PASSES):
            w1_grouped = unit_pool.tile([P, K_PASS, PACK], BF16, tag="grouped", align_bytes=64)
            nc.vector.tensor_copy(
                out=w1_grouped[:].rearrange("p (t q) j -> p t q j", t=PACK),
                in_=w1_raw[:, :, g * K_PASS : (g + 1) * K_PASS].rearrange(
                    "p j (q t) -> p t q j", t=PACK
                ),
            )
            w1_codes, w1_scales = quantise(w1_grouped, K_PASS)
            z_ps = psum.tile([P, PACK, TOKENS], F32, tag="bank")
            z_rows = z_pool.tile([P, PACK, TOKENS], BF16)
            for t in range(PACK):
                block = slice(t * P, (t + 1) * P)
                nc.tensor.matmul_mx(
                    out=z_ps[:, t, :],
                    lhsT=w1_codes[:, block].bitcast(FP8X4),
                    lhsT_scale=w1_scales[:, block],
                    rhs=x_codes[:].bitcast(FP8X4),
                    rhs_scale=x_scales[:],
                    start=True,
                    stop=True,
                )
                nc.scalar.activation(
                    out=z_rows[:, t, :],
                    in_=z_ps[:, t, :],
                    func=ACT.Tanh,
                    bias=b1_f32[:, g * PACK + t : g * PACK + t + 1],
                )
            z_grouped = z_pool.tile([P, TOKENS, PACK], BF16, align_bytes=64)
            nc.vector.tensor_copy(out=z_grouped[:], in_=z_rows[:].rearrange("p t m -> p m t"))
            nc.vector.quantize_mx(
                out=z_codes[:, g, :].bitcast(FP8X4),
                scales=z_scales[:, g, :],
                in_=z_grouped[:].rearrange("p m t -> p (m t)"),
            )

        def unit_product(raw_passes, u, label, scalar_cols):
            banks = [
                psum.tile([P, BANK_COLS], F32, tag="bank", name="%s_acc%d" % (label, b))
                for b in range(UNIT_BANKS)
            ]
            vector_cols = UNIT_COLS - scalar_cols
            for g in range(HIDDEN_PASSES):
                rows = raw_passes[g][:, :, u * UNIT_COLS : (u + 1) * UNIT_COLS]
                grouped = unit_pool.tile([P, UNIT_COLS, PACK], BF16, align_bytes=64)
                nc.vector.tensor_copy(
                    out=grouped[:, :vector_cols, :].rearrange("p (n i) j -> p n j i", i=4),
                    in_=rows[:, :, :vector_cols].rearrange("p j (n i) -> p n j i", i=4),
                )
                if scalar_cols > 0:
                    nc.scalar.copy(
                        out=grouped[:, vector_cols:, :].rearrange("p (n i) j -> p n j i", i=4),
                        in_=rows[:, :, vector_cols:].rearrange("p j (n i) -> p n j i", i=4),
                    )
                codes, scales = quantise(grouped, UNIT_COLS)
                for b in range(UNIT_BANKS):
                    cols = slice(b * BANK_COLS, (b + 1) * BANK_COLS)
                    nc.tensor.matmul_mx(
                        out=banks[b][:],
                        lhsT=z_codes[:, g, :].bitcast(FP8X4),
                        lhsT_scale=z_scales[:, g, :],
                        rhs=codes[:, cols].bitcast(FP8X4),
                        rhs_scale=scales[:, cols],
                        start=(g == 0),
                        stop=(g == HIDDEN_PASSES - 1),
                    )
            return banks

        sigma_flat = out_1.rearrange("b k i j -> b (k i j)")
        bank_chunks = BANK_COLS // CHUNK_DIAG
        for u in range(PASS_UNITS):
            sig_banks = unit_product(wsig_raw, u, "sig", WSIG_SCALAR_COLS)
            for b in range(UNIT_BANKS):
                c = u * UNIT_BANKS + b
                sig_pre = const.tile([P, BANK_COLS], F32, name="sig_pre%d" % c)
                nc.vector.tensor_tensor(
                    out=sig_pre[:],
                    in0=sig_banks[b][:],
                    in1=bias_all[:, BSIG_AT + c * BANK_COLS : BSIG_AT + (c + 1) * BANK_COLS],
                    op=ALU.add,
                )
                for h in range(bank_chunks):
                    chunk = c * bank_chunks + h
                    buf = sigma_bufs[chunk % SIGMA_BUFS]
                    diagonals = buf[:].rearrange("p (k e) -> p k e", e=DIMS * DIMS)[
                        :, :, 0 : DIMS * DIMS : DIMS + 1
                    ]
                    nc.scalar.activation(
                        out=diagonals,
                        in_=sig_pre[:, h * CHUNK_DIAG : (h + 1) * CHUNK_DIAG].rearrange(
                            "p (k i) -> p k i", i=DIMS
                        ),
                        func=ACT.Exp,
                    )
                    nc.scalar.dma_start(
                        out=sigma_flat[:, chunk * CHUNK_COLS : (chunk + 1) * CHUNK_COLS],
                        in_=buf[:],
                    )

        wpi_grouped = const.tile([P, HIDDEN_PASSES, COMPONENTS, PACK], BF16, align_bytes=64)
        nc.vector.tensor_copy(out=wpi_grouped[:], in_=wpi_raw[:].rearrange("p g j n -> p g n j"))
        wpi_codes = const.tile([P, HIDDEN_PASSES, COMPONENTS], U32, align_bytes=64)
        wpi_scales = const.tile([P, HIDDEN_PASSES, COMPONENTS], U8, align_bytes=64)
        pi_ps = psum.tile([P, COMPONENTS], F32, tag="bank")
        for g in range(HIDDEN_PASSES):
            nc.vector.quantize_mx(
                out=wpi_codes[:, g, :].bitcast(FP8X4),
                scales=wpi_scales[:, g, :],
                in_=wpi_grouped[:, g, :, :].rearrange("p n j -> p (n j)"),
            )
            nc.tensor.matmul_mx(
                out=pi_ps[:],
                lhsT=z_codes[:, g, :].bitcast(FP8X4),
                lhsT_scale=z_scales[:, g, :],
                rhs=wpi_codes[:, g, :].bitcast(FP8X4),
                rhs_scale=wpi_scales[:, g, :],
                start=(g == 0),
                stop=(g == HIDDEN_PASSES - 1),
            )
        logits = const.tile([P, COMPONENTS], F32)
        nc.vector.tensor_tensor(
            out=logits[:], in0=pi_ps[:], in1=bias_all[:, BPI_AT : BPI_AT + COMPONENTS], op=ALU.add
        )
        top = const.tile([P, 1], F32)
        nc.vector.reduce_max(out=top[:], in_=logits[:], axis=AXIS.X)
        minus_top = const.tile([P, 1], F32)
        nc.vector.tensor_scalar_mul(out=minus_top[:], in0=top[:], scalar1=-1.0)
        weights = const.tile([P, COMPONENTS], F32)
        total = const.tile([P, 1], F32)
        nc.scalar.activation(
            out=weights[:], in_=logits[:], func=ACT.Exp, bias=minus_top[:], accum_out=total[:]
        )
        inverse = const.tile([P, 1], F32)
        nc.vector.reciprocal(out=inverse[:], in_=total[:])
        pi_sb = const.tile([P, COMPONENTS], F32)
        nc.vector.tensor_scalar_mul(out=pi_sb[:], in0=weights[:], scalar1=inverse[:])
        nc.sync.dma_start(out=out_0, in_=pi_sb[:])

        mu_sb = const.tile([P, HEAD_COLS], F32)
        for u in range(PASS_UNITS):
            mu_banks = unit_product(wmu_raw, u, "mu", 0)
            for b in range(UNIT_BANKS):
                c = u * UNIT_BANKS + b
                nc.vector.tensor_tensor(
                    out=mu_sb[:, c * BANK_COLS : (c + 1) * BANK_COLS],
                    in0=mu_banks[b][:],
                    in1=bias_all[:, BMU_AT + c * BANK_COLS : BMU_AT + (c + 1) * BANK_COLS],
                    op=ALU.add,
                )
        nc.sync.dma_start(out=out_2.rearrange("b k i -> b (k i)"), in_=mu_sb[:])
